import numpy as np
import ml_dtypes


def mxq(x, axis, fmt="e4m3"):
    dtype, down = {"e4m3": (ml_dtypes.float8_e4m3fn, 7), "e5m2": (ml_dtypes.float8_e5m2, 14)}[fmt]
    v = np.moveaxis(np.asarray(x, np.float32).astype(ml_dtypes.bfloat16).astype(np.float64), axis, -1)
    blocks = v.reshape(v.shape[:-1] + (-1, 32))
    amax = np.abs(blocks).max(-1, keepdims=True)
    byte = np.maximum(np.where(amax > 0, np.frexp(amax)[1] - 1 + 127, 0) - down, 1)
    scale = np.exp2(byte - 127.0)
    codes = (blocks / scale).astype(np.float32).astype(dtype).astype(np.float64)
    return np.moveaxis((codes * scale).reshape(v.shape), -1, axis)


WIDE = False


def mx_kscale(k):
    if not WIDE:
        return np.ones(k)
    levels = np.array([10, -10, 5, -5, 0])
    if k % 512:
        return np.exp2(np.random.permutation(np.resize(levels, k // 32))).repeat(32)
    a = np.empty((k // 512, 16))
    for p in range(k // 512):
        a[p, :8] = np.random.permutation(np.resize(levels, 8))
        for g in range(8):
            far = levels[np.abs(levels - a[p, g]) >= 10]
            a[p, g + 8] = far[np.random.randint(len(far))]
    return np.exp2(a.ravel()).repeat(32)


BF16 = ml_dtypes.bfloat16


def bf(x):
    return np.asarray(x, np.float32).astype(BF16)


def f64(x):
    return np.asarray(x).astype(np.float64)


B, K, NH, N = 512, 2048, 4096, 1024
EPSILON = 0.1


def setup_inputs():
    s = mx_kscale(K)
    g = 1.0 / np.mean(1.0 / s)
    return {"x": bf(np.random.standard_normal((B, K)) * s),
            "y": bf(np.random.standard_normal((B, N)) * 12.0 / np.sqrt(K) * g),
            "beta": bf(np.random.random((K, N)) * 1.7 / np.sqrt(K) / s[:, None]),
            "bias_lin": bf(np.random.standard_normal(N) * 0.1),
            "W1": bf(-np.random.random((NH, K)) * 1.7 / np.sqrt(K) / s[None, :]),
            "W2": bf(np.random.random((N, NH)) * (0.5 + np.random.random((N, 1))) * 2.0 / NH**2),
            "bias1": bf(np.random.standard_normal(NH) * 0.1),
            "bias2": bf(np.random.standard_normal(N) * 0.1),
            "adv": 1}


def core(x, y, beta, bias_lin, W1, W2, bias1, bias2, adv):
    xq = mxq(f64(x), 1, "e4m3")
    lin = (xq @ mxq(f64(beta), 0, "e4m3")) + f64(bias_lin)
    if adv:
        beta_norm = np.sum(np.abs(f64(beta)), axis=0)
        lin = lin - EPSILON * f64(y) * beta_norm
    if adv:
        one = NH * np.sum(f64(W2), axis=1) + f64(bias2)
        one = np.broadcast_to(one, lin.shape)
    else:
        h = np.maximum((xq @ mxq(f64(W1), 1, "e4m3").T) + f64(bias1), 0.0)
        one = (mxq(h, 1, "e4m3") @ mxq(f64(W2), 1, "e4m3").T) + f64(bias2)
    return lin + one


def e4m3fn_bytes(y):
    return np.clip(np.asarray(y, np.float64), -448.0, 448.0).astype(np.float32).astype(ml_dtypes.float8_e4m3fn).view(np.uint8)


Y_SCALE = 120.0


def reference(x, y, beta, bias_lin, W1, W2, bias1, bias2, adv):
    out = core(x, y, beta, bias_lin, W1, W2, bias1, bias2, adv)
    return out, e4m3fn_bytes(out * Y_SCALE)

@@ -1,0 +1,413 @@
+from contextlib import ExitStack
+
+import concourse.masks as masks
+import concourse.mybir as mybir
+
+B, K, NH, N = 512, 2048, 4096, 1024
+FLOPS = 2 * B * K * N
+BYTES = 2 * (B * K + B * N + K * N + N * NH + 2 * N) + 4 * B * N + B * N
+
+F32 = mybir.dt.float32
+BF16 = mybir.dt.bfloat16
+I32 = mybir.dt.int32
+U32 = mybir.dt.uint32
+U8 = mybir.dt.uint8
+FP8X4 = mybir.dt.float8_e4m3fn_x4
+FP8 = mybir.dt.float8_e4m3fn
+ALU = mybir.AluOpType
+ACT = mybir.ActivationFunctionType
+AX = mybir.AxisListType
+
+P = 128
+NBT = B // P
+NG = K // 512
+NJT = N // P
+VW = 2176
+PT = ()
+
+
+def tile_advresnet_kernel(tc, x, y, beta, bias_lin, W1, W2, bias1, bias2, adv, out_0, out_1):
+    nc = tc.nc
+    assert adv == 1
+
+    with ExitStack() as ctx:
+        const = ctx.enter_context(tc.tile_pool(name="const", bufs=1))
+        keep = ctx.enter_context(tc.tile_pool(name="keep", bufs=1))
+        rotp = ctx.enter_context(tc.tile_pool(name="rotp", bufs=2))
+        psum = ctx.enter_context(tc.psum_pool(name="psum", bufs=1))
+        ctx.enter_context(tc.manual_schedule())
+
+        btile = const.tile([P, P], BF16, name="btile")
+        ident = const.tile([P, P], F32, name="ident")
+        ident_bf = const.tile([P, P], BF16, name="ident_bf")
+        ones = const.tile([P, 2], BF16, name="ones")
+        warm = const.tile([P, 1], F32, name="warm")
+        bcol = const.tile([P, 16], F32, name="bcol")
+        bsum = const.tile([P, NJT], F32, name="bsum")
+        bn_col = const.tile([P, NJT], F32, name="bn_col")
+        sel = const.tile([P, 16], BF16, name="sel")
+        sel_f = const.tile([P, 16], F32, name="sel_f")
+        ones_f = const.tile([P, 2], F32, name="ones_f")
+        sv = const.tile([P, NJT], F32, name="sv")
+        ss = const.tile([P, NJT], F32, name="ss")
+
+        masks.make_identity(nc, ident[:])
+        nc.vector.memset(ones[:], 1.0)
+        nc.vector.memset(btile[:], 0.0)
+        nc.vector.memset(ones_f[:], 1.0)
+        nc.scalar.activation(out=warm[:], in_=ones[:, 0:1], func=ACT.Copy)
+
+        state = {}
+        x_sb = [keep.tile([P, K], BF16, name="x_sb%d" % t) for t in range(NBT)]
+        y_sb = keep.tile([P, NBT, N], BF16, name="y_sb")
+
+        def load_beta(g):
+            raw = rotp.tile([P, 4, N], BF16, name="raw", tag="big", bufs=8)
+            nc.sync.dma_start(out=raw[:], in_=beta[512 * g:512 * (g + 1), :].rearrange("(p t) j -> p t j", t=4))
+            state["raw%d" % g] = raw
+
+        def load_x(t):
+            nc.sync.dma_start(out=x_sb[t][:], in_=x[P * t:P * (t + 1), :])
+
+        def load_w2(j):
+            w = rotp.tile([P, NH], BF16, name="w2t", tag="big", bufs=8)
+            nc.sync.dma_start(out=w[:], in_=W2[P * j:P * (j + 1), :])
+            state["w2%d" % j] = w
+
+        def load_w2p(j):
+            w = rotp.tile([P, 8, 512], BF16, name="w2p", tag="big", bufs=8)
+            nc.sync.dma_start(out=w[:], in_=W2[P * j:P * (j + 1), :].rearrange("(J a) (c e) -> (a c) J e", a=16, c=8))
+            state["w2%d" % j] = w
+
+        def load_bias():
+            nc.sync.dma_start(out=btile[0:8, :], in_=bias_lin.rearrange("(c p) -> c p", p=P))
+            nc.sync.dma_start(out=btile[8:16, :], in_=bias2.rearrange("(c p) -> c p", p=P))
+
+        def load_y():
+            nc.sync.dma_start(out=y_sb[:], in_=y.rearrange("(t p) j -> p t j", p=P))
+
+        xc = [keep.tile([P, 512], U32, name="xc%d" % t, align_bytes=64) for t in range(NBT)]
+        xs = [keep.tile([P, 512], U8, name="xs%d" % t, align_bytes=64) for t in range(NBT)]
+        bc = [keep.tile([P, N], U32, name="bc%d" % g, align_bytes=64) for g in range(NG)]
+        bs = [keep.tile([P, N], U8, name="bs%d" % g, align_bytes=64) for g in range(NG)]
+        pall = [keep.tile([P, NBT, 512], F32, name="pall%d" % h) for h in range(2)]
+        bnb = keep.tile([P, 2, 512], F32, name="bnb")
+        o45 = keep.tile([P, NBT, 256], F32, name="o45")
+        o67 = keep.tile([P, NBT, 256], F32, name="o67")
+        f8h0 = keep.tile([P, NBT, 512], FP8, name="f8h0")
+        f845 = keep.tile([P, NBT, 256], FP8, name="f845")
+        f867 = keep.tile([P, NBT, 256], FP8, name="f867")
+        out0v = out_0.rearrange("(t p) j -> p t j", p=P)
+        out1v = out_1.rearrange("(t p) j -> p t j", p=P)
+
+        def abs_beta(g):
+            ab = rotp.tile([P, 4, N], BF16, name="ab", tag="ab", bufs=3)
+            nc.vector.tensor_scalar(out=ab[:].bitcast(I32), in0=state["raw%d" % g][:].bitcast(I32),
+                                    scalar1=0x7FFF7FFF, scalar2=None, op0=ALU.bitwise_and)
+            state["ab%d" % g] = ab
+
+        def ilv(g, h):
+            gt = rotp.tile([P, 512, 4], BF16, name="g%d" % h, tag="g%d" % h, bufs=2, align_bytes=64)
+            dst = gt[:].rearrange("p (c i) t -> p c t i", i=4)
+            src = state["raw%d" % g][:, :, 512 * h:512 * (h + 1)].rearrange("p t (c i) -> p c t i", i=4)
+            if h == 0:
+                nc.vector.tensor_copy(out=dst, in_=src)
+            else:
+                nc.scalar.copy(out=dst, in_=src)
+            state["g%d%d" % (g, h)] = gt
+
+        def quant_beta(g, h):
+            gt = state["g%d%d" % (g, h)]
+            nc.vector.quantize_mx(out=bc[g][:, 512 * h:512 * (h + 1)].bitcast(FP8X4),
+                                  scales=bs[g][:, 512 * h:512 * (h + 1)],
+                                  in_=gt[:].rearrange("p j t -> p (j t)"))
+
+        def bn_mm(g, j0, j1):
+            ab = state["ab%d" % g]
+            bn_ps = state["bn_ps"]
+            for j in range(j0, j1):
+                for t in range(4):
+                    nc.tensor.matmul(out=bn_ps[:, 4 * j + g:4 * j + g + 1], lhsT=ab[:, t, P * j:P * (j + 1)],
+                                     rhs=ones[:, 0:1], start=(t == 0), stop=(t == 3))
+
+        def x_tr(t, half):
+            words = x_sb[t][:].bitcast(F32)
+            if half == 0:
+                state["gx%d" % t] = rotp.tile([P, NG, P, 2], F32, name="gx", tag="gx", bufs=2, align_bytes=64)
+            xt = psum.tile([P, 2, 2, P], F32, name="xt", tag="rot", bufs=3)
+            for gg in range(2):
+                g = 2 * half + gg
+                for u in range(2):
+                    nc.tensor.transpose(xt[:, gg, u, :], words[:, 256 * g + u:256 * (g + 1):2], ident[:])
+            state["xt%d%d" % (t, half)] = xt
+
+        def x_cp(t, half):
+            nc.scalar.copy(out=state["gx%d" % t][:, 2 * half:2 * half + 2, :, :],
+                           in_=state["xt%d%d" % (t, half)][:].rearrange("p g u b -> p g b u"))
+
+        def quant_x(t):
+            gx = state["gx%d" % t]
+            nc.vector.quantize_mx(out=xc[t][:].bitcast(FP8X4), scales=xs[t][:],
+                                  in_=gx[:].rearrange("p g b u -> p (g b u)").bitcast(BF16))
+
+        def red_v(j):
+            w = state["w2%d" % j]
+            nc.vector.tensor_scalar(out=w[:, 0:VW], in0=w[:, 0:VW], scalar1=4096.0, scalar2=None,
+                                    op0=ALU.mult, op1=ALU.add, accum_out=sv[:, j:j + 1])
+
+        def red_s(j):
+            w = state["w2%d" % j]
+            nc.scalar.activation(out=w[:, VW:NH], in_=w[:, VW:NH], func=ACT.Copy, scale=4096.0,
+                                 accum_out=ss[:, j:j + 1])
+
+        def spread_c(dst, j):
+            parts = (sv, bsum) if j in PT else (sv, ss, bsum)
+            for n in range(len(parts)):
+                nc.tensor.matmul(out=dst, lhsT=parts[n][:, j:j + 1].to_broadcast([P, P]), rhs=ident[:],
+                                 is_transpose=True, start=(n == 0), stop=(n == len(parts) - 1))
+
+        def make_sel():
+            nc.vector.tensor_reduce(out=sel_f[:], in_=ident[:].rearrange("p (n e) -> p n e", e=8), axis=AX.X, op=ALU.add)
+            nc.vector.tensor_copy(out=sel[:], in_=sel_f[:])
+
+        def s1_mm(j):
+            w = state["w2%d" % j]
+            s1 = psum.tile([P, P], F32, name="s1", tag="s1", bufs=1)
+            for jj in range(8):
+                for mc in range(4):
+                    nc.tensor.matmul(out=s1[:, 16 * jj:16 * jj + 16], lhsT=w[:, jj, P * mc:P * (mc + 1)], rhs=sel[:],
+                                     start=(mc == 0), stop=(mc == 3))
+            state["s1%d" % j] = s1
+
+        def s1_copy(j):
+            s1sb = rotp.tile([P, P], F32, name="s1sb", tag="s1sb", bufs=2)
+            nc.scalar.activation(out=s1sb[:], in_=state["s1%d" % j][:], func=ACT.Copy, scale=4096.0)
+            state["s1sb%d" % j] = s1sb
+
+        def s_part(j):
+            nc.tensor.matmul(out=state["bn_ps"][:, 32 + j:33 + j], lhsT=state["s1sb%d" % j][:], rhs=ones_f[:, 0:1],
+                             start=True, stop=True)
+
+        def s_copy(j):
+            nc.vector.tensor_copy(out=sv[:, j:j + 1], in_=state["bn_ps"][:, 32 + j:33 + j])
+
+        def c_bc(j):
+            cbc = psum.tile([P, P], F32, name="cbc", tag="rot", bufs=3)
+            spread_c(cbc[:], j)
+            state["cbc%d" % j] = cbc
+
+        def cb_h0():
+            cb = psum.tile([P, 4, P], F32, name="cb", tag="rot", bufs=3)
+            for q in range(4):
+                spread_c(cb[:, q, :], q)
+            state["cb"] = cb
+
+        def bb_t(h):
+            bb = psum.tile([P, 4, P], F32, name="bb", tag="rot", bufs=3)
+            for q in range(4):
+                j = 4 * h + q
+                nc.tensor.transpose(bb[:, q, :], bn_col[:, j:j + 1].to_broadcast([P, P]), ident[:])
+            state["bb%d" % h] = bb
+
+        def bb_c(h):
+            nc.scalar.activation(out=bnb[:, h, :], in_=state["bb%d" % h][:].rearrange("p q j -> p (q j)"), func=ACT.Copy,
+                                 scale=-0.1)
+
+        def t1(h, t):
+            nc.gpsimd.tensor_tensor(out=pall[h][:, t, :], in0=y_sb[:, t, 512 * h:512 * (h + 1)], in1=bnb[:, h, :],
+                                    op=ALU.mult)
+
+        def mx(h, t):
+            acc = psum.tile([P, 512], F32, name="acc", tag="acc", bufs=4)
+            for g in range(NG):
+                nc.tensor.matmul_mx(out=acc[:],
+                                    lhsT=xc[t][:, P * g:P * (g + 1)].bitcast(FP8X4),
+                                    lhsT_scale=xs[t][:, P * g:P * (g + 1)],
+                                    rhs=bc[g][:, 512 * h:512 * (h + 1)].bitcast(FP8X4),
+                                    rhs_scale=bs[g][:, 512 * h:512 * (h + 1)],
+                                    start=(g == 0), stop=(g == NG - 1))
+            state["acc%d%d" % (h, t)] = acc
+
+        def p_add(h, t):
+            nc.vector.tensor_tensor(out=pall[h][:, t, :], in0=state["acc%d%d" % (h, t)][:], in1=pall[h][:, t, :],
+                                    op=ALU.add)
+
+        def oh(t):
+            nc.vector.tensor_tensor(out=pall[0][:, t, :], in0=pall[0][:, t, :],
+                                    in1=state["cb"][:].rearrange("p q j -> p (q j)"), op=ALU.add)
+
+        def o_add(j, dst):
+            nc.vector.tensor_tensor(out=dst, in0=pall[1][:, :, P * (j - 4):P * (j - 3)],
+                                    in1=state["cbc%d" % j][:].unsqueeze(1).to_broadcast([P, NBT, P]), op=ALU.add)
+
+        def cast_s(src, f8t):
+            nc.scalar.activation(out=f8t.rearrange("p t j -> p (t j)"), in_=src.rearrange("p t j -> p (t j)"),
+                                 func=ACT.Copy, scale=120.0, saturate=False)
+
+        def cast_v(src, f8t):
+            nc.vector.tensor_scalar(out=f8t.rearrange("p t j -> p (t j)"), in0=src.rearrange("p t j -> p (t j)"),
+                                    scalar1=120.0, scalar2=None, op0=ALU.mult, saturate=False)
+
+        def store0(src, c0, c1):
+            nc.sync.dma_start(out=out0v[:, :, c0:c1], in_=src)
+
+        def store1(f8t, c0, c1):
+            nc.sync.dma_start(out=out1v[:, :, c0:c1], in_=f8t.bitcast(U8))
+
+        def ident_cast():
+            nc.vector.tensor_copy(out=ident_bf[:], in_=ident[:])
+
+        def bias_t():
+            state["bias_ps"] = psum.tile([P, P], BF16, name="bias_ps", tag="acc", bufs=4)
+            nc.tensor.transpose(state["bias_ps"][:], btile[:], ident_bf[:])
+
+        def bias_copy():
+            nc.vector.tensor_copy(out=bcol[:], in_=state["bias_ps"][:, 0:16])
+
+        def bias_sum():
+            nc.vector.tensor_tensor(out=bsum[:], in0=bcol[:, 0:8], in1=bcol[:, 8:16], op=ALU.add)
+
+        def bn_red(h):
+            nc.vector.tensor_reduce(out=bn_col[:, 4 * h:4 * h + 4],
+                                    in_=state["bn_ps"][:, 16 * h:16 * h + 16].rearrange("p (j g) -> p j g", g=NG),
+                                    axis=AX.X, op=ALU.add)
+
+        state["bn_ps"] = psum.tile([P, 5 * NJT], F32, name="bn_ps", tag="bn", bufs=1)
+
+        load_beta(0)
+        load_x(0)
+        load_bias()
+        load_x(1)
+        load_beta(1)
+        load_x(2)
+        load_x(3)
+        load_beta(2)
+        ident_cast()
+        load_beta(3)
+        ilv(0, 0)
+        ilv(0, 1)
+        load_y()
+        x_tr(0, 0)
+        load_w2(0)
+        abs_beta(0)
+        bias_t()
+        x_tr(0, 1)
+        load_w2(1)
+        x_tr(1, 0)
+        quant_beta(0, 0)
+        x_cp(0, 1)
+        bn_mm(0, 0, 8)
+        bias_copy()
+        quant_beta(0, 1)
+        x_cp(0, 0)
+        bias_sum()
+        x_cp(1, 0)
+        quant_x(0)
+        load_w2(2)
+        ilv(1, 1)
+        ilv(1, 0)
+        x_tr(1, 1)
+        load_w2(3)
+        x_tr(2, 0)
+        abs_beta(1)
+        x_tr(2, 1)
+        load_w2(4)
+        quant_beta(1, 0)
+        bn_mm(1, 0, 8)
+        x_cp(1, 1)
+        quant_beta(1, 1)
+        x_cp(2, 1)
+        quant_x(1)
+        x_cp(2, 0)
+        load_w2(5)
+        abs_beta(2)
+        ilv(2, 1)
+        x_tr(3, 0)
+        x_tr(3, 1)
+        ilv(2, 0)
+        bn_mm(2, 0, 8)
+        ilv(3, 0)
+        ilv(3, 1)
+        load_w2(6)
+        quant_beta(2, 0)
+        abs_beta(3)
+        quant_beta(2, 1)
+        bn_mm(3, 0, 4)
+        x_cp(3, 1)
+        load_w2(7)
+        quant_beta(3, 1)
+        x_cp(3, 0)
+        bn_mm(3, 4, 8)
+        red_v(0)
+        red_s(0)
+        bn_red(0)
+        quant_x(3)
+        bb_t(0)
+        quant_beta(3, 0)
+        bb_c(0)
+        red_v(1)
+        mx(0, 0)
+        red_s(1)
+        t1(0, 0)
+        mx(0, 1)
+        red_v(2)
+        t1(0, 2)
+        red_s(2)
+        quant_x(2)
+        t1(0, 3)
+        bn_red(1)
+        mx(0, 2)
+        red_v(3)
+        bb_t(1)
+        red_s(3)
+        p_add(0, 0)
+        t1(0, 1)
+        mx(0, 3)
+        p_add(0, 2)
+        red_v(4)
+        mx(1, 0)
+        bb_c(1)
+        cb_h0()
+        p_add(0, 3)
+        red_s(4)
+        t1(1, 1)
+        red_v(5)
+        t1(1, 3)
+        p_add(0, 1)
+        red_s(5)
+        c_bc(4)
+        oh(3)
+        mx(1, 1)
+        oh(1)
+        t1(1, 2)
+        oh(0)
+        mx(1, 2)
+        p_add(1, 1)
+        red_s(6)
+        t1(1, 0)
+        c_bc(5)
+        red_v(7)
+        mx(1, 3)
+        p_add(1, 0)
+        cast_s(pall[0][:, 0:2, :], f8h0[:, 0:2, :])
+        oh(2)
+        p_add(1, 3)
+        store0(pall[0][:], 0, 512)
+        cast_s(pall[0][:, 2:4, :], f8h0[:, 2:4, :])
+        p_add(1, 2)
+        red_v(6)
+        red_s(7)
+        store1(f8h0[:], 0, 512)
+        o_add(4, o45[:, :, 0:P])
+        c_bc(6)
+        o_add(5, o45[:, :, P:2 * P])
+        c_bc(7)
+        o_add(6, o67[:, :, 0:P])
+        cast_s(o45[:], f845[:])
+        store0(o45[:], 512, 768)
+        o_add(7, o67[:, :, P:2 * P])
+        cast_v(o67[:, 2:4, :], f867[:, 2:4, :])
+        cast_s(o67[:, 0:2, :], f867[:, 0:2, :])
+        store0(o67[:], 768, 1024)
+        store1(f845[:], 512, 768)
+        store1(f867[:], 768, 1024)

@@ -23,7 +23,10 @@ NBT = B // P
 NG = K // 512
 NJT = N // P
 VW = 2176
-PT = ()
+VW_LAST = 2688
+PT = (5, 6)
+SA = 32
+SC = P // SA
 
 
 def tile_advresnet_kernel(tc, x, y, beta, bias_lin, W1, W2, bias1, bias2, adv, out_0, out_1):
@@ -45,9 +48,9 @@ def tile_advresnet_kernel(tc, x, y, beta, bias_lin, W1, W2, bias1, bias2, adv, o
         bcol = const.tile([P, 16], F32, name="bcol")
         bsum = const.tile([P, NJT], F32, name="bsum")
         bn_col = const.tile([P, NJT], F32, name="bn_col")
-        sel = const.tile([P, 16], BF16, name="sel")
-        sel_f = const.tile([P, 16], F32, name="sel_f")
-        ones_f = const.tile([P, 2], F32, name="ones_f")
+        sel = const.tile([P, SA], BF16, name="sel")
+        sel_f = const.tile([P, SA], F32, name="sel_f")
+        ones_f = const.tile([P, P], F32, name="ones_f")
         sv = const.tile([P, NJT], F32, name="sv")
         ss = const.tile([P, NJT], F32, name="ss")
 
@@ -61,22 +64,23 @@ def tile_advresnet_kernel(tc, x, y, beta, bias_lin, W1, W2, bias1, bias2, adv, o
         x_sb = [keep.tile([P, K], BF16, name="x_sb%d" % t) for t in range(NBT)]
         y_sb = keep.tile([P, NBT, N], BF16, name="y_sb")
 
-        def load_beta(g):
+        def load_beta(g, parts):
             raw = rotp.tile([P, 4, N], BF16, name="raw", tag="big", bufs=8)
-            nc.sync.dma_start(out=raw[:], in_=beta[512 * g:512 * (g + 1), :].rearrange("(p t) j -> p t j", t=4))
+            src = beta[512 * g:512 * (g + 1), :].rearrange("(p t) j -> p t j", t=4)
+            for (c0, c1) in parts:
+                nc.sync.dma_start(out=raw[:, :, c0:c1], in_=src[:, :, c0:c1])
             state["raw%d" % g] = raw
 
         def load_x(t):
             nc.sync.dma_start(out=x_sb[t][:], in_=x[P * t:P * (t + 1), :])
 
         def load_w2(j):
-            w = rotp.tile([P, NH], BF16, name="w2t", tag="big", bufs=8)
-            nc.sync.dma_start(out=w[:], in_=W2[P * j:P * (j + 1), :])
-            state["w2%d" % j] = w
-
-        def load_w2p(j):
-            w = rotp.tile([P, 8, 512], BF16, name="w2p", tag="big", bufs=8)
-            nc.sync.dma_start(out=w[:], in_=W2[P * j:P * (j + 1), :].rearrange("(J a) (c e) -> (a c) J e", a=16, c=8))
+            if j in PT:
+                w = rotp.tile([P, P // SA, NH // SC], BF16, name="w2p", tag="big", bufs=8)
+                nc.sync.dma_start(out=w[:], in_=W2[P * j:P * (j + 1), :].rearrange("(J a) (c e) -> (a c) J e", a=SA, c=SC))
+            else:
+                w = rotp.tile([P, NH], BF16, name="w2t", tag="big", bufs=8)
+                nc.sync.dma_start(out=w[:], in_=W2[P * j:P * (j + 1), :])
             state["w2%d" % j] = w
 
         def load_bias():
@@ -106,14 +110,15 @@ def tile_advresnet_kernel(tc, x, y, beta, bias_lin, W1, W2, bias1, bias2, adv, o
                                     scalar1=0x7FFF7FFF, scalar2=None, op0=ALU.bitwise_and)
             state["ab%d" % g] = ab
 
-        def ilv(g, h):
+        def ilv(g, h, parts=((0, 512),)):
             gt = rotp.tile([P, 512, 4], BF16, name="g%d" % h, tag="g%d" % h, bufs=2, align_bytes=64)
-            dst = gt[:].rearrange("p (c i) t -> p c t i", i=4)
-            src = state["raw%d" % g][:, :, 512 * h:512 * (h + 1)].rearrange("p t (c i) -> p c t i", i=4)
-            if h == 0:
-                nc.vector.tensor_copy(out=dst, in_=src)
-            else:
-                nc.scalar.copy(out=dst, in_=src)
+            for (c0, c1) in parts:
+                dst = gt[:, c0:c1, :].rearrange("p (c i) t -> p c t i", i=4)
+                src = state["raw%d" % g][:, :, 512 * h + c0:512 * h + c1].rearrange("p t (c i) -> p c t i", i=4)
+                if h == 0:
+                    nc.vector.tensor_copy(out=dst, in_=src)
+                else:
+                    nc.scalar.copy(out=dst, in_=src)
             state["g%d%d" % (g, h)] = gt
 
         def quant_beta(g, h):
@@ -133,7 +138,7 @@ def tile_advresnet_kernel(tc, x, y, beta, bias_lin, W1, W2, bias1, bias2, adv, o
         def x_tr(t, half):
             words = x_sb[t][:].bitcast(F32)
             if half == 0:
-                state["gx%d" % t] = rotp.tile([P, NG, P, 2], F32, name="gx", tag="gx", bufs=2, align_bytes=64)
+                state["gx%d" % t] = rotp.tile([P, NG, P, 2], F32, name="gx", tag="gx", bufs=4, align_bytes=64)
             xt = psum.tile([P, 2, 2, P], F32, name="xt", tag="rot", bufs=3)
             for gg in range(2):
                 g = 2 * half + gg
@@ -150,33 +155,38 @@ def tile_advresnet_kernel(tc, x, y, beta, bias_lin, W1, W2, bias1, bias2, adv, o
             nc.vector.quantize_mx(out=xc[t][:].bitcast(FP8X4), scales=xs[t][:],
                                   in_=gx[:].rearrange("p g b u -> p (g b u)").bitcast(BF16))
 
-        def red_v(j):
+        def red_v(j, vw=VW):
             w = state["w2%d" % j]
-            nc.vector.tensor_scalar(out=w[:, 0:VW], in0=w[:, 0:VW], scalar1=4096.0, scalar2=None,
+            nc.vector.tensor_scalar(out=w[:, 0:vw], in0=w[:, 0:vw], scalar1=4096.0, scalar2=None,
                                     op0=ALU.mult, op1=ALU.add, accum_out=sv[:, j:j + 1])
 
-        def red_s(j):
+        def red_s(j, vw=VW):
             w = state["w2%d" % j]
-            nc.scalar.activation(out=w[:, VW:NH], in_=w[:, VW:NH], func=ACT.Copy, scale=4096.0,
+            nc.scalar.activation(out=w[:, vw:NH], in_=w[:, vw:NH], func=ACT.Copy, scale=4096.0,
                                  accum_out=ss[:, j:j + 1])
 
         def spread_c(dst, j):
-            parts = (sv, bsum) if j in PT else (sv, ss, bsum)
+            if j in PT:
+                nc.tensor.matmul(out=dst, lhsT=ones_f[:], rhs=state["s1sb%d" % j][:], start=True, stop=False)
+                parts = (bsum,)
+            else:
+                parts = (sv, ss, bsum)
             for n in range(len(parts)):
                 nc.tensor.matmul(out=dst, lhsT=parts[n][:, j:j + 1].to_broadcast([P, P]), rhs=ident[:],
-                                 is_transpose=True, start=(n == 0), stop=(n == len(parts) - 1))
+                                 is_transpose=True, start=(n == 0 and j not in PT), stop=(n == len(parts) - 1))
 
         def make_sel():
-            nc.vector.tensor_reduce(out=sel_f[:], in_=ident[:].rearrange("p (n e) -> p n e", e=8), axis=AX.X, op=ALU.add)
+            nc.vector.tensor_reduce(out=sel_f[:], in_=ident[:].rearrange("p (n e) -> p n e", e=SC), axis=AX.X, op=ALU.add)
             nc.vector.tensor_copy(out=sel[:], in_=sel_f[:])
 
         def s1_mm(j):
             w = state["w2%d" % j]
-            s1 = psum.tile([P, P], F32, name="s1", tag="s1", bufs=1)
-            for jj in range(8):
-                for mc in range(4):
-                    nc.tensor.matmul(out=s1[:, 16 * jj:16 * jj + 16], lhsT=w[:, jj, P * mc:P * (mc + 1)], rhs=sel[:],
-                                     start=(mc == 0), stop=(mc == 3))
+            s1 = psum.tile([P, P], F32, name="s1", tag="acc", bufs=4)
+            nm = NH // SC // P
+            for jj in range(P // SA):
+                for mc in range(nm):
+                    nc.tensor.matmul(out=s1[:, SA * jj:SA * (jj + 1)], lhsT=w[:, jj, P * mc:P * (mc + 1)], rhs=sel[:],
+                                     start=(mc == 0), stop=(mc == nm - 1))
             state["s1%d" % j] = s1
 
         def s1_copy(j):
@@ -274,140 +284,133 @@ def tile_advresnet_kernel(tc, x, y, beta, bias_lin, W1, W2, bias1, bias2, adv, o
 
         state["bn_ps"] = psum.tile([P, 5 * NJT], F32, name="bn_ps", tag="bn", bufs=1)
 
-        load_beta(0)
+        Q = ((0, 256), (256, 512))
+        load_beta(0, ((0, 256), (512, 768), (256, 512), (768, 1024)))
+        load_beta(1, ((0, N),))
         load_x(0)
         load_bias()
+        load_beta(2, ((0, N),))
         load_x(1)
-        load_beta(1)
         load_x(2)
+        load_beta(3, ((0, N),))
         load_x(3)
-        load_beta(2)
-        ident_cast()
-        load_beta(3)
-        ilv(0, 0)
-        ilv(0, 1)
         load_y()
-        x_tr(0, 0)
-        load_w2(0)
+        for j in range(4):
+            load_w2(j)
+        ident_cast()
+        make_sel()
+
+        ilv(0, 0, Q)
+        ilv(0, 1, Q)
         abs_beta(0)
+        load_w2(4)
+        bn_mm(0, 0, 8)
+        quant_beta(0, 0)
+        quant_beta(0, 1)
+        abs_beta(1)
+        ilv(1, 0)
+        ilv(1, 1)
+        load_w2(5)
+        x_tr(0, 0)
         bias_t()
         x_tr(0, 1)
-        load_w2(1)
-        x_tr(1, 0)
-        quant_beta(0, 0)
-        x_cp(0, 1)
-        bn_mm(0, 0, 8)
-        bias_copy()
-        quant_beta(0, 1)
-        x_cp(0, 0)
-        bias_sum()
-        x_cp(1, 0)
-        quant_x(0)
-        load_w2(2)
-        ilv(1, 1)
-        ilv(1, 0)
-        x_tr(1, 1)
-        load_w2(3)
-        x_tr(2, 0)
-        abs_beta(1)
-        x_tr(2, 1)
-        load_w2(4)
-        quant_beta(1, 0)
         bn_mm(1, 0, 8)
-        x_cp(1, 1)
+        quant_beta(1, 0)
+        bias_copy()
+        bias_sum()
+        x_cp(0, 0)
+        x_cp(0, 1)
         quant_beta(1, 1)
-        x_cp(2, 1)
-        quant_x(1)
-        x_cp(2, 0)
-        load_w2(5)
         abs_beta(2)
-        ilv(2, 1)
-        x_tr(3, 0)
-        x_tr(3, 1)
         ilv(2, 0)
+        ilv(2, 1)
+        load_w2(6)
+        x_tr(1, 0)
+        x_tr(1, 1)
         bn_mm(2, 0, 8)
+        quant_x(0)
+        quant_beta(2, 0)
+        x_cp(1, 0)
+        x_cp(1, 1)
+        quant_beta(2, 1)
+        x_tr(2, 0)
+        x_tr(2, 1)
+        x_tr(3, 0)
+        abs_beta(3)
         ilv(3, 0)
         ilv(3, 1)
-        load_w2(6)
-        quant_beta(2, 0)
-        abs_beta(3)
-        quant_beta(2, 1)
-        bn_mm(3, 0, 4)
-        x_cp(3, 1)
         load_w2(7)
-        quant_beta(3, 1)
-        x_cp(3, 0)
+        bn_mm(3, 0, 4)
         bn_mm(3, 4, 8)
+        x_cp(2, 0)
+        x_cp(2, 1)
+        x_cp(3, 0)
+        quant_x(1)
+        bn_red(0)
+        quant_beta(3, 0)
+        bn_red(1)
+        bb_t(0)
+        x_tr(3, 1)
+        bb_t(1)
+        bb_c(0)
+        x_cp(3, 1)
+        bb_c(1)
+        quant_x(2)
+        quant_beta(3, 1)
+        quant_x(3)
+
+        for h in range(2):
+            for t in range(NBT):
+                t1(h, t)
+        for t in range(NBT):
+            mx(0, t)
+        p_add(0, 0)
+        mx(1, 0)
         red_v(0)
         red_s(0)
-        bn_red(0)
-        quant_x(3)
-        bb_t(0)
-        quant_beta(3, 0)
-        bb_c(0)
-        red_v(1)
-        mx(0, 0)
-        red_s(1)
-        t1(0, 0)
-        mx(0, 1)
-        red_v(2)
-        t1(0, 2)
-        red_s(2)
-        quant_x(2)
-        t1(0, 3)
-        bn_red(1)
-        mx(0, 2)
-        red_v(3)
-        bb_t(1)
-        red_s(3)
-        p_add(0, 0)
-        t1(0, 1)
-        mx(0, 3)
-        p_add(0, 2)
-        red_v(4)
-        mx(1, 0)
-        bb_c(1)
-        cb_h0()
-        p_add(0, 3)
-        red_s(4)
-        t1(1, 1)
-        red_v(5)
-        t1(1, 3)
         p_add(0, 1)
-        red_s(5)
-        c_bc(4)
-        oh(3)
         mx(1, 1)
-        oh(1)
-        t1(1, 2)
-        oh(0)
+        red_v(1)
+        red_s(1)
+        p_add(0, 2)
         mx(1, 2)
-        p_add(1, 1)
-        red_s(6)
-        t1(1, 0)
-        c_bc(5)
-        red_v(7)
+        p_add(0, 3)
         mx(1, 3)
+        red_v(2)
+        red_s(2)
+        red_v(3)
+        red_s(3)
+        cb_h0()
         p_add(1, 0)
-        cast_s(pall[0][:, 0:2, :], f8h0[:, 0:2, :])
-        oh(2)
-        p_add(1, 3)
-        store0(pall[0][:], 0, 512)
-        cast_s(pall[0][:, 2:4, :], f8h0[:, 2:4, :])
+        p_add(1, 1)
+        red_v(4)
+        red_s(4)
+        c_bc(4)
         p_add(1, 2)
-        red_v(6)
-        red_s(7)
+        p_add(1, 3)
+        for t in range(NBT):
+            oh(t)
+        store0(pall[0][:], 0, 512)
+        s1_mm(5)
+        cast_s(pall[0][:, 0:2, :], f8h0[:, 0:2, :])
+        s1_copy(5)
+        cast_s(pall[0][:, 2:4, :], f8h0[:, 2:4, :])
         store1(f8h0[:], 0, 512)
+        s1_mm(6)
+        c_bc(5)
         o_add(4, o45[:, :, 0:P])
+        s1_copy(6)
         c_bc(6)
+        red_v(7, VW_LAST)
+        red_s(7, VW_LAST)
         o_add(5, o45[:, :, P:2 * P])
-        c_bc(7)
-        o_add(6, o67[:, :, 0:P])
-        cast_s(o45[:], f845[:])
         store0(o45[:], 512, 768)
+        cast_s(o45[:], f845[:])
+        store1(f845[:], 512, 768)
+        o_add(6, o67[:, :, 0:P])
+        c_bc(7)
         o_add(7, o67[:, :, P:2 * P])
+        store0(o67[:], 768, 1024)
         cast_v(o67[:, 2:4, :], f867[:, 2:4, :])
         cast_s(o67[:, 0:2, :], f867[:, 0:2, :])
-        store0(o67[:], 768, 1024)
-        store1(f845[:], 512, 768)
         store1(f867[:], 768, 1024)

@@ -25,7 +25,7 @@ NJT = N // P
 VW = 2176
 VW_LAST = 2688
 PT = (5, 6)
-SA = 32
+SA = 64
 SC = P // SA
 
 
@@ -61,18 +61,18 @@ def tile_advresnet_kernel(tc, x, y, beta, bias_lin, W1, W2, bias1, bias2, adv, o
         nc.scalar.activation(out=warm[:], in_=ones[:, 0:1], func=ACT.Copy)
 
         state = {}
-        x_sb = [keep.tile([P, K], BF16, name="x_sb%d" % t) for t in range(NBT)]
+        x_sb = keep.tile([P, NBT, K], BF16, name="x_sb")
         y_sb = keep.tile([P, NBT, N], BF16, name="y_sb")
 
         def load_beta(g, parts):
             raw = rotp.tile([P, 4, N], BF16, name="raw", tag="big", bufs=8)
             src = beta[512 * g:512 * (g + 1), :].rearrange("(p t) j -> p t j", t=4)
-            for (c0, c1) in parts:
-                nc.sync.dma_start(out=raw[:, :, c0:c1], in_=src[:, :, c0:c1])
+            for (t0, t1_) in parts:
+                nc.sync.dma_start(out=raw[:, t0:t1_, :], in_=src[:, t0:t1_, :])
             state["raw%d" % g] = raw
 
-        def load_x(t):
-            nc.sync.dma_start(out=x_sb[t][:], in_=x[P * t:P * (t + 1), :])
+        def load_x(t0):
+            nc.sync.dma_start(out=x_sb[:, t0:t0 + 2, :], in_=x.rearrange("(p t) k -> p t k", t=NBT)[:, t0:t0 + 2, :])
 
         def load_w2(j):
             if j in PT:
@@ -88,7 +88,7 @@ def tile_advresnet_kernel(tc, x, y, beta, bias_lin, W1, W2, bias1, bias2, adv, o
             nc.sync.dma_start(out=btile[8:16, :], in_=bias2.rearrange("(c p) -> c p", p=P))
 
         def load_y():
-            nc.sync.dma_start(out=y_sb[:], in_=y.rearrange("(t p) j -> p t j", p=P))
+            nc.sync.dma_start(out=y_sb[:], in_=y.rearrange("(p t) j -> p t j", t=NBT))
 
         xc = [keep.tile([P, 512], U32, name="xc%d" % t, align_bytes=64) for t in range(NBT)]
         xs = [keep.tile([P, 512], U8, name="xs%d" % t, align_bytes=64) for t in range(NBT)]
@@ -101,13 +101,14 @@ def tile_advresnet_kernel(tc, x, y, beta, bias_lin, W1, W2, bias1, bias2, adv, o
         f8h0 = keep.tile([P, NBT, 512], FP8, name="f8h0")
         f845 = keep.tile([P, NBT, 256], FP8, name="f845")
         f867 = keep.tile([P, NBT, 256], FP8, name="f867")
-        out0v = out_0.rearrange("(t p) j -> p t j", p=P)
-        out1v = out_1.rearrange("(t p) j -> p t j", p=P)
+        out0v = out_0.rearrange("(p t) j -> p t j", t=NBT)
+        out1v = out_1.rearrange("(p t) j -> p t j", t=NBT)
 
-        def abs_beta(g):
+        def abs_beta(g, parts=((0, 4),)):
             ab = rotp.tile([P, 4, N], BF16, name="ab", tag="ab", bufs=3)
-            nc.vector.tensor_scalar(out=ab[:].bitcast(I32), in0=state["raw%d" % g][:].bitcast(I32),
-                                    scalar1=0x7FFF7FFF, scalar2=None, op0=ALU.bitwise_and)
+            for (t0, t1_) in parts:
+                nc.vector.tensor_scalar(out=ab[:, t0:t1_, :].bitcast(I32), in0=state["raw%d" % g][:, t0:t1_, :].bitcast(I32),
+                                        scalar1=0x7FFF7FFF, scalar2=None, op0=ALU.bitwise_and)
             state["ab%d" % g] = ab
 
         def ilv(g, h, parts=((0, 512),)):
@@ -136,7 +137,7 @@ def tile_advresnet_kernel(tc, x, y, beta, bias_lin, W1, W2, bias1, bias2, adv, o
                                      rhs=ones[:, 0:1], start=(t == 0), stop=(t == 3))
 
         def x_tr(t, half):
-            words = x_sb[t][:].bitcast(F32)
+            words = x_sb[:, t, :].bitcast(F32)
             if half == 0:
                 state["gx%d" % t] = rotp.tile([P, NG, P, 2], F32, name="gx", tag="gx", bufs=4, align_bytes=64)
             xt = psum.tile([P, 2, 2, P], F32, name="xt", tag="rot", bufs=3)
@@ -284,25 +285,24 @@ def tile_advresnet_kernel(tc, x, y, beta, bias_lin, W1, W2, bias1, bias2, adv, o
 
         state["bn_ps"] = psum.tile([P, 5 * NJT], F32, name="bn_ps", tag="bn", bufs=1)
 
-        Q = ((0, 256), (256, 512))
-        load_beta(0, ((0, 256), (512, 768), (256, 512), (768, 1024)))
-        load_beta(1, ((0, N),))
+        HALVES = ((0, 2), (2, 4))
+        WHOLE = ((0, 4),)
+        load_beta(0, HALVES)
+        load_beta(1, WHOLE)
         load_x(0)
         load_bias()
-        load_beta(2, ((0, N),))
-        load_x(1)
+        load_beta(2, WHOLE)
         load_x(2)
-        load_beta(3, ((0, N),))
-        load_x(3)
+        load_beta(3, WHOLE)
         load_y()
         for j in range(4):
             load_w2(j)
         ident_cast()
         make_sel()
 
-        ilv(0, 0, Q)
-        ilv(0, 1, Q)
-        abs_beta(0)
+        abs_beta(0, HALVES)
+        ilv(0, 0)
+        ilv(0, 1)
         load_w2(4)
         bn_mm(0, 0, 8)
         quant_beta(0, 0)

@@ -105,22 +105,24 @@ def tile_advresnet_kernel(tc, x, y, beta, bias_lin, W1, W2, bias1, bias2, adv, o
         out1v = out_1.rearrange("(p t) j -> p t j", t=NBT)
 
         def abs_beta(g, parts=((0, 4),)):
-            ab = rotp.tile([P, 4, N], BF16, name="ab", tag="ab", bufs=3)
+            if ("ab%d" % g) not in state:
+                state["ab%d" % g] = rotp.tile([P, 4, N], BF16, name="ab", tag="ab", bufs=3)
+            ab = state["ab%d" % g]
             for (t0, t1_) in parts:
                 nc.vector.tensor_scalar(out=ab[:, t0:t1_, :].bitcast(I32), in0=state["raw%d" % g][:, t0:t1_, :].bitcast(I32),
                                         scalar1=0x7FFF7FFF, scalar2=None, op0=ALU.bitwise_and)
-            state["ab%d" % g] = ab
 
-        def ilv(g, h, parts=((0, 512),)):
-            gt = rotp.tile([P, 512, 4], BF16, name="g%d" % h, tag="g%d" % h, bufs=2, align_bytes=64)
-            for (c0, c1) in parts:
-                dst = gt[:, c0:c1, :].rearrange("p (c i) t -> p c t i", i=4)
-                src = state["raw%d" % g][:, :, 512 * h + c0:512 * h + c1].rearrange("p t (c i) -> p c t i", i=4)
+        def ilv(g, h, parts=((0, 4),)):
+            if ("g%d%d" % (g, h)) not in state:
+                state["g%d%d" % (g, h)] = rotp.tile([P, 512, 4], BF16, name="g%d" % h, tag="g%d" % h, bufs=2, align_bytes=64)
+            gt = state["g%d%d" % (g, h)]
+            for (t0, t1_) in parts:
+                dst = gt[:, :, t0:t1_].rearrange("p (c i) t -> p c t i", i=4)
+                src = state["raw%d" % g][:, t0:t1_, 512 * h:512 * (h + 1)].rearrange("p t (c i) -> p c t i", i=4)
                 if h == 0:
                     nc.vector.tensor_copy(out=dst, in_=src)
                 else:
                     nc.scalar.copy(out=dst, in_=src)
-            state["g%d%d" % (g, h)] = gt
 
         def quant_beta(g, h):
             gt = state["g%d%d" % (g, h)]
@@ -292,8 +294,8 @@ def tile_advresnet_kernel(tc, x, y, beta, bias_lin, W1, W2, bias1, bias2, adv, o
         load_x(0)
         load_bias()
         load_beta(2, WHOLE)
-        load_x(2)
         load_beta(3, WHOLE)
+        load_x(2)
         load_y()
         for j in range(4):
             load_w2(j)
@@ -306,78 +308,78 @@ def tile_advresnet_kernel(tc, x, y, beta, bias_lin, W1, W2, bias1, bias2, adv, o
         load_w2(4)
         bn_mm(0, 0, 8)
         quant_beta(0, 0)
-        quant_beta(0, 1)
         abs_beta(1)
         ilv(1, 0)
         ilv(1, 1)
         load_w2(5)
+        quant_beta(0, 1)
         x_tr(0, 0)
         bias_t()
         x_tr(0, 1)
         bn_mm(1, 0, 8)
         quant_beta(1, 0)
         bias_copy()
-        bias_sum()
         x_cp(0, 0)
         x_cp(0, 1)
         quant_beta(1, 1)
         abs_beta(2)
+        bias_sum()
         ilv(2, 0)
         ilv(2, 1)
-        load_w2(6)
+        load_w2(7)
         x_tr(1, 0)
         x_tr(1, 1)
         bn_mm(2, 0, 8)
-        quant_x(0)
+        abs_beta(3)
         quant_beta(2, 0)
         x_cp(1, 0)
         x_cp(1, 1)
         quant_beta(2, 1)
+        bn_mm(3, 0, 4)
+        bn_mm(3, 4, 8)
+        ilv(3, 0)
+        ilv(3, 1)
+        load_w2(6)
+        quant_x(0)
         x_tr(2, 0)
         x_tr(2, 1)
         x_tr(3, 0)
-        abs_beta(3)
-        ilv(3, 0)
-        ilv(3, 1)
-        load_w2(7)
-        bn_mm(3, 0, 4)
-        bn_mm(3, 4, 8)
-        x_cp(2, 0)
-        x_cp(2, 1)
-        x_cp(3, 0)
-        quant_x(1)
-        bn_red(0)
         quant_beta(3, 0)
+        bn_red(0)
         bn_red(1)
+        x_cp(2, 0)
         bb_t(0)
+        x_cp(2, 1)
         x_tr(3, 1)
+        x_cp(3, 0)
         bb_t(1)
         bb_c(0)
         x_cp(3, 1)
         bb_c(1)
-        quant_x(2)
         quant_beta(3, 1)
-        quant_x(3)
+        quant_x(1)
+        quant_x(2)
 
         for h in range(2):
             for t in range(NBT):
                 t1(h, t)
+        red_v(0)
+        quant_x(3)
         for t in range(NBT):
             mx(0, t)
+        red_s(0)
         p_add(0, 0)
         mx(1, 0)
-        red_v(0)
-        red_s(0)
-        p_add(0, 1)
-        mx(1, 1)
         red_v(1)
         red_s(1)
+        p_add(0, 1)
+        mx(1, 1)
         p_add(0, 2)
         mx(1, 2)
-        p_add(0, 3)
-        mx(1, 3)
         red_v(2)
         red_s(2)
+        p_add(0, 3)
+        mx(1, 3)
         red_v(3)
         red_s(3)
         cb_h0()
@@ -385,31 +387,31 @@ def tile_advresnet_kernel(tc, x, y, beta, bias_lin, W1, W2, bias1, bias2, adv, o
         p_add(1, 1)
         red_v(4)
         red_s(4)
+        s1_mm(5)
         c_bc(4)
-        p_add(1, 2)
-        p_add(1, 3)
         for t in range(NBT):
             oh(t)
         store0(pall[0][:], 0, 512)
-        s1_mm(5)
-        cast_s(pall[0][:, 0:2, :], f8h0[:, 0:2, :])
+        p_add(1, 2)
+        p_add(1, 3)
         s1_copy(5)
-        cast_s(pall[0][:, 2:4, :], f8h0[:, 2:4, :])
-        store1(f8h0[:], 0, 512)
-        s1_mm(6)
         c_bc(5)
-        o_add(4, o45[:, :, 0:P])
-        s1_copy(6)
-        c_bc(6)
         red_v(7, VW_LAST)
         red_s(7, VW_LAST)
+        s1_mm(6)
+        c_bc(7)
+        cast_s(pall[0][:, 0:2, :], f8h0[:, 0:2, :])
+        cast_s(pall[0][:, 2:4, :], f8h0[:, 2:4, :])
+        store1(f8h0[:], 0, 512)
+        o_add(4, o45[:, :, 0:P])
         o_add(5, o45[:, :, P:2 * P])
         store0(o45[:], 512, 768)
+        o_add(7, o67[:, :, P:2 * P])
+        s1_copy(6)
+        c_bc(6)
         cast_s(o45[:], f845[:])
         store1(f845[:], 512, 768)
         o_add(6, o67[:, :, 0:P])
-        c_bc(7)
-        o_add(7, o67[:, :, P:2 * P])
         store0(o67[:], 768, 1024)
         cast_v(o67[:, 2:4, :], f867[:, 2:4, :])
         cast_s(o67[:, 0:2, :], f867[:, 0:2, :])

@@ -253,6 +253,16 @@ def tile_advresnet_kernel(tc, x, y, beta, bias_lin, W1, W2, bias1, bias2, adv, o
             nc.vector.tensor_tensor(out=dst, in0=pall[1][:, :, P * (j - 4):P * (j - 3)],
                                     in1=state["cbc%d" % j][:].unsqueeze(1).to_broadcast([P, NBT, P]), op=ALU.add)
 
+        def warm_bf(n):
+            dps = psum.tile([P, 512], F32, name="dps", tag="acc", bufs=4)
+            for i in range(n):
+                nc.tensor.matmul(out=dps[:], lhsT=ident_bf[:], rhs=x_sb[:, 0, 512 * i:512 * (i + 1)], start=True, stop=True)
+
+        def warm_f32(t):
+            if t == 0:
+                state["dpf"] = psum.tile([P, 256], F32, name="dpf", tag="bn", bufs=1)
+            nc.tensor.matmul(out=state["dpf"][:], lhsT=ident[:], rhs=pall[0][:, t, 0:256], start=True, stop=True)
+
         def cast_s(src, f8t):
             nc.scalar.activation(out=f8t.rearrange("p t j -> p (t j)"), in_=src.rearrange("p t j -> p (t j)"),
                                  func=ACT.Copy, scale=120.0, saturate=False)
@@ -297,11 +307,12 @@ def tile_advresnet_kernel(tc, x, y, beta, bias_lin, W1, W2, bias1, bias2, adv, o
         load_beta(3, WHOLE)
         load_x(2)
         load_y()
-        for j in range(4):
-            load_w2(j)
+        load_w2(0)
+        load_w2(1)
+        load_w2(2)
+        load_w2(3)
         ident_cast()
         make_sel()
-
         abs_beta(0, HALVES)
         ilv(0, 0)
         ilv(0, 1)
@@ -344,6 +355,7 @@ def tile_advresnet_kernel(tc, x, y, beta, bias_lin, W1, W2, bias1, bias2, adv, o
         x_tr(2, 0)
         x_tr(2, 1)
         x_tr(3, 0)
+        warm_bf(2)
         quant_beta(3, 0)
         bn_red(0)
         bn_red(1)
@@ -359,14 +371,20 @@ def tile_advresnet_kernel(tc, x, y, beta, bias_lin, W1, W2, bias1, bias2, adv, o
         quant_beta(3, 1)
         quant_x(1)
         quant_x(2)
-
-        for h in range(2):
-            for t in range(NBT):
-                t1(h, t)
+        t1(0, 0)
+        t1(0, 1)
+        t1(0, 2)
+        t1(0, 3)
+        t1(1, 0)
+        t1(1, 1)
+        t1(1, 2)
+        t1(1, 3)
         red_v(0)
         quant_x(3)
-        for t in range(NBT):
-            mx(0, t)
+        mx(0, 0)
+        mx(0, 1)
+        mx(0, 2)
+        mx(0, 3)
         red_s(0)
         p_add(0, 0)
         mx(1, 0)
@@ -389,8 +407,10 @@ def tile_advresnet_kernel(tc, x, y, beta, bias_lin, W1, W2, bias1, bias2, adv, o
         red_s(4)
         s1_mm(5)
         c_bc(4)
-        for t in range(NBT):
-            oh(t)
+        oh(0)
+        oh(1)
+        oh(2)
+        oh(3)
         store0(pall[0][:], 0, 512)
         p_add(1, 2)
         p_add(1, 3)
@@ -398,6 +418,10 @@ def tile_advresnet_kernel(tc, x, y, beta, bias_lin, W1, W2, bias1, bias2, adv, o
         c_bc(5)
         red_v(7, VW_LAST)
         red_s(7, VW_LAST)
+        warm_f32(0)
+        warm_f32(1)
+        warm_f32(2)
+        warm_f32(3)
         s1_mm(6)
         c_bc(7)
         cast_s(pall[0][:, 0:2, :], f8h0[:, 0:2, :])

from contextlib import ExitStack

import concourse.masks as masks
import concourse.mybir as mybir

B, K, NH, N = 512, 2048, 4096, 1024
FLOPS = 2 * B * K * N
BYTES = 2 * (B * K + B * N + K * N + N * NH + 2 * N) + 4 * B * N + B * N

F32 = mybir.dt.float32
BF16 = mybir.dt.bfloat16
I32 = mybir.dt.int32
U32 = mybir.dt.uint32
U8 = mybir.dt.uint8
FP8X4 = mybir.dt.float8_e4m3fn_x4
FP8 = mybir.dt.float8_e4m3fn
ALU = mybir.AluOpType
ACT = mybir.ActivationFunctionType
AX = mybir.AxisListType

P = 128
NBT = B // P
NG = K // 512
NJT = N // P
VW = 2176
VW_LAST = 2688
PT = (5, 6)
SA = 64
SC = P // SA


def tile_advresnet_kernel(tc, x, y, beta, bias_lin, W1, W2, bias1, bias2, adv, out_0, out_1):
    nc = tc.nc
    assert adv == 1

    with ExitStack() as ctx:
        const = ctx.enter_context(tc.tile_pool(name="const", bufs=1))
        keep = ctx.enter_context(tc.tile_pool(name="keep", bufs=1))
        rotp = ctx.enter_context(tc.tile_pool(name="rotp", bufs=2))
        psum = ctx.enter_context(tc.psum_pool(name="psum", bufs=1))
        ctx.enter_context(tc.manual_schedule())

        btile = const.tile([P, P], BF16, name="btile")
        ident = const.tile([P, P], F32, name="ident")
        ident_bf = const.tile([P, P], BF16, name="ident_bf")
        ones = const.tile([P, 2], BF16, name="ones")
        warm = const.tile([P, 1], F32, name="warm")
        bcol = const.tile([P, 16], F32, name="bcol")
        bsum = const.tile([P, NJT], F32, name="bsum")
        bn_col = const.tile([P, NJT], F32, name="bn_col")
        sel = const.tile([P, SA], BF16, name="sel")
        sel_f = const.tile([P, SA], F32, name="sel_f")
        ones_f = const.tile([P, P], F32, name="ones_f")
        sv = const.tile([P, NJT], F32, name="sv")
        ss = const.tile([P, NJT], F32, name="ss")

        masks.make_identity(nc, ident[:])
        nc.vector.memset(ones[:], 1.0)
        nc.vector.memset(btile[:], 0.0)
        nc.vector.memset(ones_f[:], 1.0)
        nc.scalar.activation(out=warm[:], in_=ones[:, 0:1], func=ACT.Copy)

        state = {}
        x_sb = keep.tile([P, NBT, K], BF16, name="x_sb")
        y_sb = keep.tile([P, NBT, N], BF16, name="y_sb")

        def load_beta(g, parts):
            raw = rotp.tile([P, 4, N], BF16, name="raw", tag="big", bufs=8)
            src = beta[512 * g:512 * (g + 1), :].rearrange("(p t) j -> p t j", t=4)
            for (t0, t1_) in parts:
                nc.sync.dma_start(out=raw[:, t0:t1_, :], in_=src[:, t0:t1_, :])
            state["raw%d" % g] = raw

        def load_x(t0):
            nc.sync.dma_start(out=x_sb[:, t0:t0 + 2, :], in_=x.rearrange("(p t) k -> p t k", t=NBT)[:, t0:t0 + 2, :])

        def load_w2(j):
            if j in PT:
                w = rotp.tile([P, P // SA, NH // SC], BF16, name="w2p", tag="big", bufs=8)
                nc.sync.dma_start(out=w[:], in_=W2[P * j:P * (j + 1), :].rearrange("(J a) (c e) -> (a c) J e", a=SA, c=SC))
            else:
                w = rotp.tile([P, NH], BF16, name="w2t", tag="big", bufs=8)
                nc.sync.dma_start(out=w[:], in_=W2[P * j:P * (j + 1), :])
            state["w2%d" % j] = w

        def load_bias():
            nc.sync.dma_start(out=btile[0:8, :], in_=bias_lin.rearrange("(c p) -> c p", p=P))
            nc.sync.dma_start(out=btile[8:16, :], in_=bias2.rearrange("(c p) -> c p", p=P))

        def load_y():
            nc.sync.dma_start(out=y_sb[:], in_=y.rearrange("(p t) j -> p t j", t=NBT))

        xc = [keep.tile([P, 512], U32, name="xc%d" % t, align_bytes=64) for t in range(NBT)]
        xs = [keep.tile([P, 512], U8, name="xs%d" % t, align_bytes=64) for t in range(NBT)]
        bc = [keep.tile([P, N], U32, name="bc%d" % g, align_bytes=64) for g in range(NG)]
        bs = [keep.tile([P, N], U8, name="bs%d" % g, align_bytes=64) for g in range(NG)]
        pall = [keep.tile([P, NBT, 512], F32, name="pall%d" % h) for h in range(2)]
        bnb = keep.tile([P, 2, 512], F32, name="bnb")
        o45 = keep.tile([P, NBT, 256], F32, name="o45")
        o67 = keep.tile([P, NBT, 256], F32, name="o67")
        f8h0 = keep.tile([P, NBT, 512], FP8, name="f8h0")
        f845 = keep.tile([P, NBT, 256], FP8, name="f845")
        f867 = keep.tile([P, NBT, 256], FP8, name="f867")
        out0v = out_0.rearrange("(p t) j -> p t j", t=NBT)
        out1v = out_1.rearrange("(p t) j -> p t j", t=NBT)

        def abs_beta(g, parts=((0, 4),)):
            if ("ab%d" % g) not in state:
                state["ab%d" % g] = rotp.tile([P, 4, N], BF16, name="ab", tag="ab", bufs=3)
            ab = state["ab%d" % g]
            for (t0, t1_) in parts:
                nc.vector.tensor_scalar(out=ab[:, t0:t1_, :].bitcast(I32), in0=state["raw%d" % g][:, t0:t1_, :].bitcast(I32),
                                        scalar1=0x7FFF7FFF, scalar2=None, op0=ALU.bitwise_and)

        def ilv(g, h, parts=((0, 4),)):
            if ("g%d%d" % (g, h)) not in state:
                state["g%d%d" % (g, h)] = rotp.tile([P, 512, 4], BF16, name="g%d" % h, tag="g%d" % h, bufs=2, align_bytes=64)
            gt = state["g%d%d" % (g, h)]
            for (t0, t1_) in parts:
                dst = gt[:, :, t0:t1_].rearrange("p (c i) t -> p c t i", i=4)
                src = state["raw%d" % g][:, t0:t1_, 512 * h:512 * (h + 1)].rearrange("p t (c i) -> p c t i", i=4)
                if h == 0:
                    nc.vector.tensor_copy(out=dst, in_=src)
                else:
                    nc.scalar.copy(out=dst, in_=src)

        def quant_beta(g, h):
            gt = state["g%d%d" % (g, h)]
            nc.vector.quantize_mx(out=bc[g][:, 512 * h:512 * (h + 1)].bitcast(FP8X4),
                                  scales=bs[g][:, 512 * h:512 * (h + 1)],
                                  in_=gt[:].rearrange("p j t -> p (j t)"))

        def bn_mm(g, j0, j1):
            ab = state["ab%d" % g]
            bn_ps = state["bn_ps"]
            for j in range(j0, j1):
                for t in range(4):
                    nc.tensor.matmul(out=bn_ps[:, 4 * j + g:4 * j + g + 1], lhsT=ab[:, t, P * j:P * (j + 1)],
                                     rhs=ones[:, 0:1], start=(t == 0), stop=(t == 3))

        def x_tr(t, half):
            words = x_sb[:, t, :].bitcast(F32)
            if half == 0:
                state["gx%d" % t] = rotp.tile([P, NG, P, 2], F32, name="gx", tag="gx", bufs=4, align_bytes=64)
            xt = psum.tile([P, 2, 2, P], F32, name="xt", tag="rot", bufs=3)
            for gg in range(2):
                g = 2 * half + gg
                for u in range(2):
                    nc.tensor.transpose(xt[:, gg, u, :], words[:, 256 * g + u:256 * (g + 1):2], ident[:])
            state["xt%d%d" % (t, half)] = xt

        def x_cp(t, half):
            nc.scalar.copy(out=state["gx%d" % t][:, 2 * half:2 * half + 2, :, :],
                           in_=state["xt%d%d" % (t, half)][:].rearrange("p g u b -> p g b u"))

        def quant_x(t):
            gx = state["gx%d" % t]
            nc.vector.quantize_mx(out=xc[t][:].bitcast(FP8X4), scales=xs[t][:],
                                  in_=gx[:].rearrange("p g b u -> p (g b u)").bitcast(BF16))

        def red_v(j, vw=VW):
            w = state["w2%d" % j]
            nc.vector.tensor_scalar(out=w[:, 0:vw], in0=w[:, 0:vw], scalar1=4096.0, scalar2=None,
                                    op0=ALU.mult, op1=ALU.add, accum_out=sv[:, j:j + 1])

        def red_s(j, vw=VW):
            w = state["w2%d" % j]
            nc.scalar.activation(out=w[:, vw:NH], in_=w[:, vw:NH], func=ACT.Copy, scale=4096.0,
                                 accum_out=ss[:, j:j + 1])

        def spread_c(dst, j):
            if j in PT:
                nc.tensor.matmul(out=dst, lhsT=ones_f[:], rhs=state["s1sb%d" % j][:], start=True, stop=False)
                parts = (bsum,)
            else:
                parts = (sv, ss, bsum)
            for n in range(len(parts)):
                nc.tensor.matmul(out=dst, lhsT=parts[n][:, j:j + 1].to_broadcast([P, P]), rhs=ident[:],
                                 is_transpose=True, start=(n == 0 and j not in PT), stop=(n == len(parts) - 1))

        def make_sel():
            nc.vector.tensor_reduce(out=sel_f[:], in_=ident[:].rearrange("p (n e) -> p n e", e=SC), axis=AX.X, op=ALU.add)
            nc.vector.tensor_copy(out=sel[:], in_=sel_f[:])

        def s1_mm(j):
            w = state["w2%d" % j]
            s1 = psum.tile([P, P], F32, name="s1", tag="acc", bufs=4)
            nm = NH // SC // P
            for jj in range(P // SA):
                for mc in range(nm):
                    nc.tensor.matmul(out=s1[:, SA * jj:SA * (jj + 1)], lhsT=w[:, jj, P * mc:P * (mc + 1)], rhs=sel[:],
                                     start=(mc == 0), stop=(mc == nm - 1))
            state["s1%d" % j] = s1

        def s1_copy(j):
            s1sb = rotp.tile([P, P], F32, name="s1sb", tag="s1sb", bufs=2)
            nc.scalar.activation(out=s1sb[:], in_=state["s1%d" % j][:], func=ACT.Copy, scale=4096.0)
            state["s1sb%d" % j] = s1sb

        def s_part(j):
            nc.tensor.matmul(out=state["bn_ps"][:, 32 + j:33 + j], lhsT=state["s1sb%d" % j][:], rhs=ones_f[:, 0:1],
                             start=True, stop=True)

        def s_copy(j):
            nc.vector.tensor_copy(out=sv[:, j:j + 1], in_=state["bn_ps"][:, 32 + j:33 + j])

        def c_bc(j):
            cbc = psum.tile([P, P], F32, name="cbc", tag="rot", bufs=3)
            spread_c(cbc[:], j)
            state["cbc%d" % j] = cbc

        def cb_h0():
            cb = psum.tile([P, 4, P], F32, name="cb", tag="rot", bufs=3)
            for q in range(4):
                spread_c(cb[:, q, :], q)
            state["cb"] = cb

        def bb_t(h):
            bb = psum.tile([P, 4, P], F32, name="bb", tag="rot", bufs=3)
            for q in range(4):
                j = 4 * h + q
                nc.tensor.transpose(bb[:, q, :], bn_col[:, j:j + 1].to_broadcast([P, P]), ident[:])
            state["bb%d" % h] = bb

        def bb_c(h):
            nc.scalar.activation(out=bnb[:, h, :], in_=state["bb%d" % h][:].rearrange("p q j -> p (q j)"), func=ACT.Copy,
                                 scale=-0.1)

        def t1(h, t):
            nc.gpsimd.tensor_tensor(out=pall[h][:, t, :], in0=y_sb[:, t, 512 * h:512 * (h + 1)], in1=bnb[:, h, :],
                                    op=ALU.mult)

        def mx(h, t):
            acc = psum.tile([P, 512], F32, name="acc", tag="acc", bufs=4)
            for g in range(NG):
                nc.tensor.matmul_mx(out=acc[:],
                                    lhsT=xc[t][:, P * g:P * (g + 1)].bitcast(FP8X4),
                                    lhsT_scale=xs[t][:, P * g:P * (g + 1)],
                                    rhs=bc[g][:, 512 * h:512 * (h + 1)].bitcast(FP8X4),
                                    rhs_scale=bs[g][:, 512 * h:512 * (h + 1)],
                                    start=(g == 0), stop=(g == NG - 1))
            state["acc%d%d" % (h, t)] = acc

        def p_add(h, t):
            nc.vector.tensor_tensor(out=pall[h][:, t, :], in0=state["acc%d%d" % (h, t)][:], in1=pall[h][:, t, :],
                                    op=ALU.add)

        def oh(t):
            nc.vector.tensor_tensor(out=pall[0][:, t, :], in0=pall[0][:, t, :],
                                    in1=state["cb"][:].rearrange("p q j -> p (q j)"), op=ALU.add)

        def o_add(j, dst):
            nc.vector.tensor_tensor(out=dst, in0=pall[1][:, :, P * (j - 4):P * (j - 3)],
                                    in1=state["cbc%d" % j][:].unsqueeze(1).to_broadcast([P, NBT, P]), op=ALU.add)

        def warm_bf(n):
            dps = psum.tile([P, 512], F32, name="dps", tag="acc", bufs=4)
            for i in range(n):
                nc.tensor.matmul(out=dps[:], lhsT=ident_bf[:], rhs=x_sb[:, 0, 512 * i:512 * (i + 1)], start=True, stop=True)

        def warm_f32(t):
            if t == 0:
                state["dpf"] = psum.tile([P, 256], F32, name="dpf", tag="bn", bufs=1)
            nc.tensor.matmul(out=state["dpf"][:], lhsT=ident[:], rhs=pall[0][:, t, 0:256], start=True, stop=True)

        def cast_s(src, f8t):
            nc.scalar.activation(out=f8t.rearrange("p t j -> p (t j)"), in_=src.rearrange("p t j -> p (t j)"),
                                 func=ACT.Copy, scale=120.0, saturate=False)

        def cast_v(src, f8t):
            nc.vector.tensor_scalar(out=f8t.rearrange("p t j -> p (t j)"), in0=src.rearrange("p t j -> p (t j)"),
                                    scalar1=120.0, scalar2=None, op0=ALU.mult, saturate=False)

        def store0(src, c0, c1):
            nc.sync.dma_start(out=out0v[:, :, c0:c1], in_=src)

        def store1(f8t, c0, c1):
            nc.sync.dma_start(out=out1v[:, :, c0:c1], in_=f8t.bitcast(U8))

        def ident_cast():
            nc.vector.tensor_copy(out=ident_bf[:], in_=ident[:])

        def bias_t():
            state["bias_ps"] = psum.tile([P, P], BF16, name="bias_ps", tag="acc", bufs=4)
            nc.tensor.transpose(state["bias_ps"][:], btile[:], ident_bf[:])

        def bias_copy():
            nc.vector.tensor_copy(out=bcol[:], in_=state["bias_ps"][:, 0:16])

        def bias_sum():
            nc.vector.tensor_tensor(out=bsum[:], in0=bcol[:, 0:8], in1=bcol[:, 8:16], op=ALU.add)

        def bn_red(h):
            nc.vector.tensor_reduce(out=bn_col[:, 4 * h:4 * h + 4],
                                    in_=state["bn_ps"][:, 16 * h:16 * h + 16].rearrange("p (j g) -> p j g", g=NG),
                                    axis=AX.X, op=ALU.add)

        state["bn_ps"] = psum.tile([P, 5 * NJT], F32, name="bn_ps", tag="bn", bufs=1)

        HALVES = ((0, 2), (2, 4))
        WHOLE = ((0, 4),)
        load_beta(0, HALVES)
        load_beta(1, WHOLE)
        load_x(0)
        load_bias()
        load_beta(2, WHOLE)
        load_beta(3, WHOLE)
        load_x(2)
        load_y()
        load_w2(0)
        load_w2(1)
        load_w2(2)
        load_w2(3)
        ident_cast()
        make_sel()
        abs_beta(0, HALVES)
        ilv(0, 0)
        ilv(0, 1)
        load_w2(4)
        bn_mm(0, 0, 8)
        quant_beta(0, 0)
        abs_beta(1)
        ilv(1, 0)
        ilv(1, 1)
        load_w2(5)
        quant_beta(0, 1)
        x_tr(0, 0)
        bias_t()
        x_tr(0, 1)
        bn_mm(1, 0, 8)
        quant_beta(1, 0)
        bias_copy()
        x_cp(0, 0)
        x_cp(0, 1)
        quant_beta(1, 1)
        abs_beta(2)
        bias_sum()
        ilv(2, 0)
        ilv(2, 1)
        load_w2(7)
        x_tr(1, 0)
        x_tr(1, 1)
        bn_mm(2, 0, 8)
        abs_beta(3)
        quant_beta(2, 0)
        x_cp(1, 0)
        x_cp(1, 1)
        quant_beta(2, 1)
        bn_mm(3, 0, 4)
        bn_mm(3, 4, 8)
        ilv(3, 0)
        ilv(3, 1)
        load_w2(6)
        quant_x(0)
        x_tr(2, 0)
        x_tr(2, 1)
        x_tr(3, 0)
        warm_bf(2)
        quant_beta(3, 0)
        bn_red(0)
        bn_red(1)
        x_cp(2, 0)
        bb_t(0)
        x_cp(2, 1)
        x_tr(3, 1)
        x_cp(3, 0)
        bb_t(1)
        bb_c(0)
        x_cp(3, 1)
        bb_c(1)
        quant_beta(3, 1)
        quant_x(1)
        quant_x(2)
        t1(0, 0)
        t1(0, 1)
        t1(0, 2)
        t1(0, 3)
        t1(1, 0)
        t1(1, 1)
        t1(1, 2)
        t1(1, 3)
        red_v(0)
        quant_x(3)
        mx(0, 0)
        mx(0, 1)
        mx(0, 2)
        mx(0, 3)
        red_s(0)
        p_add(0, 0)
        mx(1, 0)
        red_v(1)
        red_s(1)
        p_add(0, 1)
        mx(1, 1)
        p_add(0, 2)
        mx(1, 2)
        red_v(2)
        red_s(2)
        p_add(0, 3)
        mx(1, 3)
        red_v(3)
        red_s(3)
        cb_h0()
        p_add(1, 0)
        p_add(1, 1)
        red_v(4)
        red_s(4)
        s1_mm(5)
        c_bc(4)
        oh(0)
        oh(1)
        oh(2)
        oh(3)
        store0(pall[0][:], 0, 512)
        p_add(1, 2)
        p_add(1, 3)
        s1_copy(5)
        c_bc(5)
        red_v(7, VW_LAST)
        red_s(7, VW_LAST)
        warm_f32(0)
        warm_f32(1)
        warm_f32(2)
        warm_f32(3)
        s1_mm(6)
        c_bc(7)
        cast_s(pall[0][:, 0:2, :], f8h0[:, 0:2, :])
        cast_s(pall[0][:, 2:4, :], f8h0[:, 2:4, :])
        store1(f8h0[:], 0, 512)
        o_add(4, o45[:, :, 0:P])
        o_add(5, o45[:, :, P:2 * P])
        store0(o45[:], 512, 768)
        o_add(7, o67[:, :, P:2 * P])
        s1_copy(6)
        c_bc(6)
        cast_s(o45[:], f845[:])
        store1(f845[:], 512, 768)
        o_add(6, o67[:, :, 0:P])
        store0(o67[:], 768, 1024)
        cast_v(o67[:, 2:4, :], f867[:, 2:4, :])
        cast_s(o67[:, 0:2, :], f867[:, 0:2, :])
        store1(f867[:], 768, 1024)
